import numpy as np
import ml_dtypes


def mxq(x, axis, fmt="e4m3"):
    dtype, down = {"e4m3": (ml_dtypes.float8_e4m3fn, 7), "e5m2": (ml_dtypes.float8_e5m2, 14)}[fmt]
    v = np.moveaxis(np.asarray(x, np.float32).astype(ml_dtypes.bfloat16).astype(np.float64), axis, -1)
    blocks = v.reshape(v.shape[:-1] + (-1, 32))
    amax = np.abs(blocks).max(-1, keepdims=True)
    byte = np.maximum(np.where(amax > 0, np.frexp(amax)[1] - 1 + 127, 0) - down, 1)
    scale = np.exp2(byte - 127.0)
    codes = (blocks / scale).astype(np.float32).astype(dtype).astype(np.float64)
    return np.moveaxis((codes * scale).reshape(v.shape), -1, axis)


WIDE = False


def mx_kscale(k):
    if not WIDE:
        return np.ones(k)
    levels = np.array([10, -10, 5, -5, 0])
    if k % 512:
        return np.exp2(np.random.permutation(np.resize(levels, k // 32))).repeat(32)
    a = np.empty((k // 512, 16))
    for p in range(k // 512):
        a[p, :8] = np.random.permutation(np.resize(levels, 8))
        for g in range(8):
            far = levels[np.abs(levels - a[p, g]) >= 10]
            a[p, g + 8] = far[np.random.randint(len(far))]
    return np.exp2(a.ravel()).repeat(32)


BF16 = ml_dtypes.bfloat16


def bf(x):
    return np.asarray(x, np.float32).astype(BF16)


def f64(x):
    return np.asarray(x).astype(np.float64)


B, CI, R, CO, H, W, D, K, PAD = 2, 512, 512, 128, 16, 16, 16, 3, 1
N = H * W * D


def draw0():
    s, u = mx_kscale(CI), mx_kscale(R)
    return {"x": bf(np.random.standard_normal((B, CI, H, W, D)) * s[None, :, None, None, None]),
            "U_k_h": bf(np.random.standard_normal((K, R)) / np.sqrt(K)),
            "U_k_w": bf(np.random.standard_normal((K, R)) / np.sqrt(K)),
            "U_k_d": bf(np.random.standard_normal((K, R)) / np.sqrt(K)),
            "U_c_in": bf(np.random.standard_normal((CI, R)) / np.sqrt(CI) / s[:, None] * u[None, :]),
            "U_c_out": bf(np.random.standard_normal((R, CO)) / np.sqrt(R) / u[:, None]),
            "bias": bf(np.random.standard_normal(CO) * 0.5)}


def core(x, U_k_h, U_k_w, U_k_d, U_c_in, U_c_out, bias):
    kh, kw, kd = f64(U_k_h), f64(U_k_w), f64(U_k_d)
    t = (mxq(f64(U_c_in), 0, "e4m3").T @ mxq(f64(x).reshape(B, CI, N), 1, "e4m3")).reshape(B, R, H, W, D)
    t = np.pad(t, ((0, 0), (0, 0), (PAD, PAD), (PAD, PAD), (PAD, PAD)))
    t = sum(t[:, :, k:k + H, :, :] * kh[k][None, :, None, None, None] for k in range(K))
    t = sum(t[:, :, :, k:k + W, :] * kw[k][None, :, None, None, None] for k in range(K))
    t = sum(t[:, :, :, :, k:k + D] * kd[k][None, :, None, None, None] for k in range(K))
    out = (mxq(f64(U_c_out), 0, "e4m3").T @ mxq(t.reshape(B, R, N), 1, "e4m3")).reshape(B, CO, H, W, D)
    return out + f64(bias)[None, :, None, None, None]


def e4m3fn_bytes(y):
    return np.clip(np.asarray(y, np.float64), -448.0, 448.0).astype(np.float32).astype(ml_dtypes.float8_e4m3fn).view(np.uint8)


def e4m3fn_values(b):
    return np.asarray(b, np.uint8).view(ml_dtypes.float8_e4m3fn).astype(np.float64)


def setup_inputs():
    d = draw0()
    x0 = np.asarray(d['x']).astype(np.float64)
    s = (np.max(np.abs(x0), axis=(0, 2, 3, 4), keepdims=True) / 448.0).astype(np.float32)
    out = {}
    for k, v in d.items():
        if k == 'x':
            out['x_bytes'] = e4m3fn_bytes(x0 / s.astype(np.float64))
            out['x_scale'] = s
        else:
            out[k] = v
    return out


def reference(x_bytes, x_scale, U_k_h, U_k_w, U_k_d, U_c_in, U_c_out, bias):
    return core(e4m3fn_values(x_bytes) * x_scale.astype(np.float64), U_k_h, U_k_w, U_k_d, U_c_in, U_c_out, bias)

@@ -1,0 +1,338 @@
+from contextlib import ExitStack
+
+import concourse.mybir as mybir
+
+F32 = mybir.dt.float32
+BF16 = mybir.dt.bfloat16
+U32 = mybir.dt.uint32
+U8 = mybir.dt.uint8
+FP8 = mybir.dt.float8_e4m3fn
+FP8X4 = mybir.dt.float8_e4m3fn_x4
+ADD = mybir.AluOpType.add
+MULT = mybir.AluOpType.mult
+MAX = mybir.AluOpType.max
+IS_LT = mybir.AluOpType.is_lt
+COPY = mybir.ActivationFunctionType.Copy
+IDENTITY = mybir.ActivationFunctionType.Identity
+
+BATCH, CI, R, CO, H, W, D = 2, 512, 512, 128, 16, 16, 16
+P = 128
+T = 4
+ROW = W * D
+VOX = H * ROW
+CH = 2 * ROW
+CPB = VOX // CH
+NCH = BATCH * CPB
+RING = 12
+WLINE = ROW + D
+DP = D + 4
+
+FLOPS = 2 * BATCH * VOX * (CI * R + R * CO) + 15 * BATCH * VOX * R
+
+
+def slot(row):
+    return (row + 1) % RING
+
+
+def tile_lowrankconv3d_pa_t_kernel(tc, x_bytes, x_scale, u_k_h, u_k_w, u_k_d, u_c_in, u_c_out, bias, out):
+    nc = tc.nc
+    x_view = x_bytes.rearrange("b (p t) h w d -> b p t (h w d)", t=T)
+    out_view = out.rearrange("b o h w d -> b o (h w d)")
+
+    with ExitStack() as ctx:
+        keep = ctx.enter_context(tc.tile_pool(name="keep", bufs=1))
+        work = ctx.enter_context(tc.tile_pool(name="work", bufs=2))
+        psum = ctx.enter_context(tc.psum_pool(name="psum", bufs=2))
+        ctx.enter_context(tc.manual_schedule())
+
+        xb = [keep.tile([P, T, VOX], U8, name="xb%d" % b, align_bytes=64) for b in range(BATCH)]
+        xs = keep.tile([P, T], F32, name="xs")
+        uin_raw = keep.tile([P, T, R], BF16, name="uin_raw")
+        uout_raw = keep.tile([P, T, CO], BF16, name="uout_raw")
+        tap_raw = [keep.tile([P, 3, T], BF16, name="tap_raw%d" % s) for s in range(3)]
+        bias_sb = keep.tile([P, 1], BF16, name="bias_sb")
+
+        def load_x(b, c0, c1):
+            nc.sync.dma_start(out=xb[b][:, :, c0:c1], in_=x_view[b][:, :, c0:c1])
+
+        load_x(0, 0, CH)
+        nc.sync.dma_start(out=uin_raw[:], in_=u_c_in.rearrange("(p j) r -> p j r", j=T))
+        load_x(0, CH, 2 * CH)
+        load_x(0, 2 * CH, 4 * CH)
+        load_x(0, 4 * CH, 8 * CH)
+        nc.scalar.dma_start(out=xs[:], in_=x_scale.rearrange("o (p t) h w d -> p (o t h w d)", t=T))
+        for s, u in enumerate((u_k_h, u_k_w, u_k_d)):
+            nc.scalar.dma_start(out=tap_raw[s][:], in_=u.rearrange("k (p t) -> p k t", t=T))
+        nc.scalar.dma_start(out=uout_raw[:], in_=u_c_out.rearrange("(p j) n -> p j n", j=T))
+        nc.scalar.dma_start(out=bias_sb[:], in_=bias.rearrange("(p o) -> p o", o=1))
+        load_x(1, 0, 4 * CH)
+        load_x(1, 4 * CH, 8 * CH)
+
+        t1 = keep.tile([P, T, RING + 1, WLINE], F32, name="t1")
+        t2 = [keep.tile([P, T, 34 * DP], F32, name="t2_%d" % i) for i in range(3)]
+        nc.gpsimd.memset(t1[:, :, :, 0:D], 0.0)
+        for i in range(3):
+            nc.gpsimd.memset(t2[i][:], 0.0)
+        warm = keep.tile([P, 2], F32, name="warm")
+        nc.vector.memset(warm[:, 0:1], 0.0)
+        nc.scalar.activation(warm[:, 1:2], warm[:, 0:1], IDENTITY)
+
+        inter_tiles, xq, banks = {}, {}, {}
+
+        def widen(c):
+            b, c0 = c // CPB, (c % CPB) * CH
+            xw = work.tile([P, T, CH], BF16, name="xw", tag="xw", bufs=2)
+            for t in range(T):
+                nc.scalar.activation(xw[:, t, :], xb[b][:, t, c0 : c0 + CH].bitcast(FP8), COPY, scale=xs[:, t : t + 1])
+            return xw
+
+        def interleave(c, xw, engine):
+            xi = work.tile([P, CH * T], BF16, name="xi", tag="xi", bufs=3, align_bytes=64)
+            dst = xi[:].rearrange("p (c i t) -> p c t i", i=4, t=T)
+            src = xw[:].rearrange("p t (c i) -> p c t i", i=4)
+            if engine == "v":
+                nc.vector.tensor_copy(out=dst, in_=src)
+            else:
+                nc.scalar.copy(dst, src)
+            inter_tiles[c] = xi
+
+        def quant_x(c):
+            codes = work.tile([P, CH], U32, name="xc", tag="xc", bufs=3, align_bytes=64)
+            scales = work.tile([P, CH], U8, name="xsc", tag="xsc", bufs=3, align_bytes=64)
+            nc.vector.quantize_mx(out=codes[:].bitcast(FP8X4), scales=scales[:], in_=inter_tiles.pop(c)[:])
+            xq[c] = (codes, scales)
+
+        xw0 = widen(0)
+        xw1 = widen(1)
+
+        uin_g = keep.tile([P, R * T], BF16, name="uin_g", align_bytes=64)
+        uin_c = keep.tile([P, R], U32, name="uin_c", align_bytes=64)
+        uin_s = keep.tile([P, R], U8, name="uin_s", align_bytes=64)
+        uout_g = keep.tile([P, CO * T], BF16, name="uout_g", align_bytes=64)
+        uout_c = keep.tile([P, CO], U32, name="uout_c", align_bytes=64)
+        uout_s = keep.tile([P, CO], U8, name="uout_s", align_bytes=64)
+        nc.vector.tensor_copy(
+            out=uin_g[:].rearrange("p (t m j) -> p t m j", t=T, j=T), in_=uin_raw[:].rearrange("p j (m t) -> p t m j", t=T)
+        )
+        interleave(0, xw0, "v")
+        nc.vector.quantize_mx(out=uin_c[:].bitcast(FP8X4), scales=uin_s[:], in_=uin_g[:])
+        quant_x(0)
+
+        hf = keep.tile([P, 3, T], F32, name="hf")
+        wd = keep.tile([P, 3, 2, T], F32, name="wd")
+        mag = keep.tile([P, 3, 2, T], F32, name="mag")
+        low = keep.tile([P, 2, T], F32, name="low")
+        mask = keep.tile([P, 2, T], F32, name="mask")
+        keepb = keep.tile([P, 2, T], F32, name="keepb")
+        mid = keep.tile([P, 2, T], F32, name="mid")
+        rec = keep.tile([P, 2, T], F32, name="rec")
+        ratio = keep.tile([P, 2, 2, T], F32, name="ratio")
+        gain = keep.tile([P, T], F32, name="gain")
+        htap = keep.tile([P, 3, T], F32, name="htap")
+        v = nc.vector
+        v.tensor_copy(out=hf[:], in_=tap_raw[0][:])
+        v.tensor_copy(out=wd[:, :, 0, :], in_=tap_raw[1][:])
+        v.tensor_copy(out=wd[:, :, 1, :], in_=tap_raw[2][:])
+        v.tensor_scalar(mag[:], wd[:], -1.0, None, op0=MULT)
+        v.tensor_tensor(out=mag[:], in0=mag[:], in1=wd[:], op=MAX)
+        v.tensor_tensor(out=low[:], in0=mag[:, 0], in1=mag[:, 1], op=MAX)
+        v.tensor_tensor(out=low[:], in0=low[:], in1=mag[:, 2], op=MAX)
+        v.tensor_scalar(low[:], low[:], 2.0**-80, 2.0**-24, op0=MAX, op1=MULT)
+        v.tensor_tensor(out=mask[:], in0=mag[:, 1], in1=low[:], op=IS_LT)
+        v.tensor_scalar(keepb[:], mask[:], -1.0, 1.0, op0=MULT, op1=ADD)
+        v.tensor_tensor(out=keepb[:], in0=keepb[:], in1=wd[:, 1], op=MULT)
+        v.tensor_tensor(out=mid[:], in0=mask[:], in1=low[:], op=MULT)
+        v.tensor_tensor(out=mid[:], in0=mid[:], in1=keepb[:], op=ADD)
+        v.reciprocal(rec[:], mid[:])
+        v.tensor_tensor(out=gain[:], in0=mid[:, 0], in1=mid[:, 1], op=MULT)
+        v.tensor_tensor(out=ratio[:, 0], in0=wd[:, 0], in1=rec[:], op=MULT)
+        v.tensor_tensor(out=ratio[:, 1], in0=wd[:, 2], in1=rec[:], op=MULT)
+        for k in range(3):
+            v.tensor_tensor(out=htap[:, k, :], in0=hf[:, k, :], in1=gain[:], op=MULT)
+
+        def project(c):
+            codes, scales = xq.pop(c)
+            for t in range(T):
+                bank = psum.tile([P, CH], F32, name="t0", tag="t0", bufs=6)
+                nc.tensor.matmul_mx(
+                    out=bank[:],
+                    lhsT=uin_c[:, t * P : (t + 1) * P].bitcast(FP8X4),
+                    lhsT_scale=uin_s[:, t * P : (t + 1) * P],
+                    rhs=codes[:].bitcast(FP8X4),
+                    rhs_scale=scales[:],
+                    start=True,
+                    stop=True,
+                )
+                banks[c, t] = bank
+
+        def rows(t, row, n):
+            s = slot(row)
+            return t1[:, t, s : s + n, D:WLINE]
+
+        def pair(ap, n):
+            return ap.rearrange("p (n q) -> p n q", n=n)
+
+        def evacuate(c):
+            hb, r0 = c % CPB, 2 * c
+            for t in range(T):
+                bank = banks[c, t]
+                if hb == 0:
+                    nc.scalar.activation(rows(t, r0, 1), pair(bank[:, 0:ROW], 1), COPY, scale=htap[:, 1, t : t + 1])
+                n = 1 if hb == CPB - 1 else 2
+                nc.scalar.activation(rows(t, r0 + 1, n), pair(bank[:, 0 : n * ROW], n), COPY, scale=htap[:, 0, t : t + 1])
+
+        def fma(out_ap, in0, scalar, in1):
+            nc.vector.scalar_tensor_tensor(out_ap, in0, scalar, in1, op0=MULT, op1=ADD)
+
+        def filter_h(c):
+            hb, r0 = c % CPB, 2 * c
+            for t in range(T):
+                bank, tap = banks[c, t], htap[:, 1, t : t + 1]
+                if hb == 0:
+                    todo = [(1, 1)]
+                elif slot(r0 + 1) == 0:
+                    todo = [(0, 1), (1, 1)]
+                else:
+                    todo = [(0, 2)]
+                for i, n in todo:
+                    dst = rows(t, r0 + i, n)
+                    fma(dst, pair(bank[:, i * ROW : (i + n) * ROW], n), tap, dst)
+            for t in range(T):
+                bank, tap = banks.pop((c, t)), htap[:, 2, t : t + 1]
+                i, n = (1, 1) if hb == 0 else (0, 2)
+                dst = rows(t, r0 - 1 + i, n)
+                fma(dst, pair(bank[:, i * ROW : (i + n) * ROW], n), tap, dst)
+
+        def unit(u):
+            return (0, 1) if u == 0 else ((2 * u - 1, 1) if u == NCH else (2 * u - 1, 2))
+
+        def t1_at(u, t, shift):
+            row, n = unit(u)
+            s = slot(row)
+            flat = t1[:, t].rearrange("p s q -> p (s q)")
+            o = s * WLINE + D + shift * D
+            return flat[:, o : o + n * WLINE].rearrange("p (n q) -> p n q", n=n)[:, :, 0:ROW].rearrange("p n (w d) -> p n w d", d=D)
+
+        def t2_at(u, t, shift):
+            n = unit(u)[1] * W
+            o = DP + shift
+            return t2[u % 3][:, t, o : o + n * DP].rearrange("p (n q) -> p n q", q=DP)[:, :, 0:D]
+
+        def filter_w(u):
+            n = unit(u)[1]
+            for k, shift in ((0, -1), (1, 1)):
+                for t in range(T):
+                    dst = t2_at(u, t, 0).rearrange("p (n w) d -> p n w d", n=n)
+                    fma(dst, t1_at(u, t, shift), ratio[:, k, 0, t : t + 1], t1_at(u, t, 0) if k == 0 else dst)
+
+        zt, gt, t3 = {}, {}, {}
+
+        def scale_d(u):
+            n = unit(u)[1] * ROW
+            g = work.tile([P, T, CH], F32, name="g", tag="g", bufs=2)
+            for t in range(T):
+                nc.scalar.activation(
+                    g[:, t, 0:n].rearrange("p (r d) -> p r d", d=D), t2_at(u, t, 1), COPY, scale=ratio[:, 1, 1, t : t + 1]
+                )
+            gt[u] = g
+
+        def filter_d(u):
+            n = unit(u)[1] * ROW
+            z = work.tile([P, T, CH], F32, name="z", tag="z", bufs=2)
+            for t in range(T):
+                fma(z[:, t, 0:n].rearrange("p (r d) -> p r d", d=D), t2_at(u, t, -1), ratio[:, 0, 1, t : t + 1], t2_at(u, t, 0))
+            zt[u] = z
+
+        def finish(u, engine, parts):
+            n = unit(u)[1] * ROW
+            z, g = zt.pop(u), gt.pop(u)
+            y = work.tile([P, CH * T], BF16, name="y", tag="y", bufs=3, align_bytes=64)
+            step = n // parts
+            for i in range(parts):
+                a, e = i * step, (i + 1) * step
+                engine.tensor_tensor(
+                    out=y[:, a * T : e * T].rearrange("p (c i t) -> p c t i", i=4, t=T),
+                    in0=z[:, :, a:e].rearrange("p t (c i) -> p c t i", i=4),
+                    in1=g[:, :, a:e].rearrange("p t (c i) -> p c t i", i=4),
+                    op=ADD,
+                )
+            t3[u] = y
+
+        yq, ot = {}, {}
+
+        def quant_t3(u):
+            n = unit(u)[1] * ROW
+            codes = work.tile([P, CH], U32, name="yc", tag="yc", bufs=2, align_bytes=64)
+            scales = work.tile([P, CH], U8, name="ysc", tag="ysc", bufs=2, align_bytes=64)
+            nc.vector.quantize_mx(out=codes[:, 0:n].bitcast(FP8X4), scales=scales[:, 0:n], in_=t3.pop(u)[:, 0 : n * T])
+            yq[u] = (codes, scales)
+
+        def expand(u):
+            n = unit(u)[1] * ROW
+            codes, scales = yq.pop(u)
+            bank = psum.tile([P, CH], F32, name="po", tag="po", bufs=2)
+            nc.tensor.matmul_mx(
+                out=bank[:, 0:n],
+                lhsT=uout_c[:].bitcast(FP8X4),
+                lhsT_scale=uout_s[:],
+                rhs=codes[:, 0:n].bitcast(FP8X4),
+                rhs_scale=scales[:, 0:n],
+                start=True,
+                stop=True,
+            )
+            ot[u] = bank
+
+        def store(u):
+            row, nr = unit(u)
+            n = nr * ROW
+            bank = ot.pop(u)
+            res = work.tile([P, CH], F32, name="res", tag="res", bufs=3)
+            nc.scalar.activation(res[:, 0:n], bank[:, 0:n], IDENTITY, bias=bias_sb[:, 0:1])
+            groups = {}
+            for i in range(nr):
+                groups.setdefault((row + i) // H, []).append(i)
+            for b, idx in groups.items():
+                o = (row + idx[0] - b * H) * ROW
+                m = len(idx) * ROW
+                nc.sync.dma_start(out=out_view[b][:, o : o + m], in_=res[:, idx[0] * ROW : idx[0] * ROW + m])
+
+        interleave(1, xw1, "v")
+        project(0)
+        evacuate(0)
+        interleave(2, widen(2), "s")
+        quant_x(1)
+        nc.vector.tensor_copy(out=uout_g[:].rearrange("p (n j) -> p n j", j=T), in_=uout_raw[:].rearrange("p j n -> p n j"))
+        nc.vector.quantize_mx(out=uout_c[:].bitcast(FP8X4), scales=uout_s[:], in_=uout_g[:])
+
+        for j in range(NCH):
+            if j >= 1:
+                finish(j - 1, nc.gpsimd, 2)
+            filter_h(j)
+            if j + 1 < NCH:
+                project(j + 1)
+            if j + 3 < NCH:
+                interleave(j + 3, widen(j + 3), "s")
+            if j + 1 < NCH:
+                evacuate(j + 1)
+            filter_w(j)
+            scale_d(j)
+            if j == NCH - 1:
+                filter_w(NCH)
+                scale_d(NCH)
+            if j >= 1:
+                quant_t3(j - 1)
+                expand(j - 1)
+            if j + 2 < NCH:
+                quant_x(j + 2)
+            filter_d(j)
+            if j >= 1:
+                store(j - 1)
+        filter_d(NCH)
+        finish(NCH - 1, nc.vector, 1)
+        finish(NCH, nc.vector, 1)
+        quant_t3(NCH - 1)
+        expand(NCH - 1)
+        quant_t3(NCH)
+        expand(NCH)
+        store(NCH - 1)
+        store(NCH)

@@ -1,6 +1,7 @@
 from contextlib import ExitStack
 
 import concourse.mybir as mybir
+from concourse.masks import make_identity
 
 F32 = mybir.dt.float32
 BF16 = mybir.dt.bfloat16
@@ -12,6 +13,7 @@ ADD = mybir.AluOpType.add
 MULT = mybir.AluOpType.mult
 MAX = mybir.AluOpType.max
 IS_LT = mybir.AluOpType.is_lt
+IS_EQ = mybir.AluOpType.is_equal
 COPY = mybir.ActivationFunctionType.Copy
 IDENTITY = mybir.ActivationFunctionType.Identity
 
@@ -26,6 +28,8 @@ NCH = BATCH * CPB
 RING = 12
 WLINE = ROW + D
 DP = D + 4
+GSHARE = 12
+PE_UNITS = range(2, 12)
 
 FLOPS = 2 * BATCH * VOX * (CI * R + R * CO) + 15 * BATCH * VOX * R
 
@@ -49,20 +53,24 @@ def tile_lowrankconv3d_pa_t_kernel(tc, x_bytes, x_scale, u_k_h, u_k_w, u_k_d, u_
         xs = keep.tile([P, T], F32, name="xs")
         uin_raw = keep.tile([P, T, R], BF16, name="uin_raw")
         uout_raw = keep.tile([P, T, CO], BF16, name="uout_raw")
-        tap_raw = [keep.tile([P, 3, T], BF16, name="tap_raw%d" % s) for s in range(3)]
+        htaps = keep.tile([P, 3, T], BF16, name="htaps")
+        wdtaps = keep.tile([P, 2, 16], BF16, name="wdtaps")
         bias_sb = keep.tile([P, 1], BF16, name="bias_sb")
 
         def load_x(b, c0, c1):
             nc.sync.dma_start(out=xb[b][:, :, c0:c1], in_=x_view[b][:, :, c0:c1])
 
+        for s, u in enumerate((u_k_w, u_k_d)):
+            nc.scalar.dma_start(
+                out=wdtaps[:, s, 0 : 3 * T].rearrange("p (k t) -> p k t", t=T), in_=u.rearrange("k (p t) -> p k t", t=T)
+            )
         load_x(0, 0, CH)
         nc.sync.dma_start(out=uin_raw[:], in_=u_c_in.rearrange("(p j) r -> p j r", j=T))
         load_x(0, CH, 2 * CH)
         load_x(0, 2 * CH, 4 * CH)
         load_x(0, 4 * CH, 8 * CH)
         nc.scalar.dma_start(out=xs[:], in_=x_scale.rearrange("o (p t) h w d -> p (o t h w d)", t=T))
-        for s, u in enumerate((u_k_h, u_k_w, u_k_d)):
-            nc.scalar.dma_start(out=tap_raw[s][:], in_=u.rearrange("k (p t) -> p k t", t=T))
+        nc.scalar.dma_start(out=htaps[:], in_=u_k_h.rearrange("k (p t) -> p k t", t=T))
         nc.scalar.dma_start(out=uout_raw[:], in_=u_c_out.rearrange("(p j) n -> p j n", j=T))
         nc.scalar.dma_start(out=bias_sb[:], in_=bias.rearrange("(p o) -> p o", o=1))
         load_x(1, 0, 4 * CH)
@@ -72,17 +80,21 @@ def tile_lowrankconv3d_pa_t_kernel(tc, x_bytes, x_scale, u_k_h, u_k_w, u_k_d, u_
         t2 = [keep.tile([P, T, 34 * DP], F32, name="t2_%d" % i) for i in range(3)]
         nc.gpsimd.memset(t1[:, :, :, 0:D], 0.0)
         for i in range(3):
-            nc.gpsimd.memset(t2[i][:], 0.0)
+            nc.gpsimd.memset(t2[i][:].rearrange("p t (r q) -> p t r q", q=DP)[:, :, :, D:DP], 0.0)
+        ident = keep.tile([P, P], F32, name="ident")
+        make_identity(nc, ident[:])
         warm = keep.tile([P, 2], F32, name="warm")
         nc.vector.memset(warm[:, 0:1], 0.0)
         nc.scalar.activation(warm[:, 1:2], warm[:, 0:1], IDENTITY)
 
         inter_tiles, xq, banks = {}, {}, {}
 
-        def widen(c):
+        def widen(c, vector_from=T):
             b, c0 = c // CPB, (c % CPB) * CH
             xw = work.tile([P, T, CH], BF16, name="xw", tag="xw", bufs=2)
-            for t in range(T):
+            for t in range(vector_from, T):
+                nc.vector.tensor_scalar(xw[:, t, :], xb[b][:, t, c0 : c0 + CH].bitcast(FP8), xs[:, t : t + 1], None, op0=MULT)
+            for t in range(vector_from):
                 nc.scalar.activation(xw[:, t, :], xb[b][:, t, c0 : c0 + CH].bitcast(FP8), COPY, scale=xs[:, t : t + 1])
             return xw
 
@@ -102,7 +114,37 @@ def tile_lowrankconv3d_pa_t_kernel(tc, x_bytes, x_scale, u_k_h, u_k_w, u_k_d, u_
             nc.vector.quantize_mx(out=codes[:].bitcast(FP8X4), scales=scales[:], in_=inter_tiles.pop(c)[:])
             xq[c] = (codes, scales)
 
-        xw0 = widen(0)
+        mag = keep.tile([P, 2, 3, T], F32, name="mag")
+        low = keep.tile([P, 2, T], F32, name="low")
+        mask = keep.tile([P, 2, T], F32, name="mask")
+        mid = keep.tile([P, 2, T], F32, name="mid")
+        fill = keep.tile([P, 2, T], F32, name="fill")
+        rec = keep.tile([P, 2, T], F32, name="rec")
+        ratio = keep.tile([P, 2, 2, T], F32, name="ratio")
+        gain = keep.tile([P, T], F32, name="gain")
+        htap = keep.tile([P, 3, T], F32, name="htap")
+        v = nc.vector
+        wd = wdtaps[:, :, 0 : 3 * T].rearrange("p s (k t) -> p s k t", t=T)
+        for s in range(2):
+            v.scalar_tensor_tensor(mag[:, s], wd[:, s], -1.0, wd[:, s], op0=MULT, op1=MAX)
+        v.tensor_tensor(out=low[:], in0=mag[:, :, 0], in1=mag[:, :, 2], op=MAX)
+        v.tensor_scalar(low[:], low[:], 2.0**-80, 2.0**-24, op0=MAX, op1=MULT)
+        v.tensor_tensor(out=mask[:], in0=mag[:, :, 1], in1=low[:], op=IS_LT)
+        v.scalar_tensor_tensor(mid[:], mask[:], 0.0, wd[:, :, 1], op0=IS_EQ, op1=MULT)
+        v.tensor_tensor(out=fill[:], in0=mask[:], in1=low[:], op=MULT)
+        v.tensor_tensor(out=mid[:], in0=mid[:], in1=fill[:], op=ADD)
+        v.reciprocal(rec[:], mid[:])
+        g = nc.gpsimd
+        g.tensor_tensor(out=gain[:], in0=mid[:, 0], in1=mid[:, 1], op=MULT)
+        for k in (1, 0, 2):
+            g.tensor_tensor(out=htap[:, k, :], in0=htaps[:, k, :], in1=gain[:], op=MULT)
+        for i, k in enumerate((0, 2)):
+            g.tensor_tensor(out=ratio[:, i], in0=wd[:, :, k], in1=rec[:], op=MULT)
+        diag = [keep.tile([P, P], F32, name="diag%d" % i) for i in range(2)]
+        for i in range(2):
+            g.tensor_scalar(diag[i][:], ident[:], ratio[:, i, 0, 0:1], 0.0, op0=MULT, op1=ADD)
+
+        xw0 = widen(0, 2)
         xw1 = widen(1)
 
         uin_g = keep.tile([P, R * T], BF16, name="uin_g", align_bytes=64)
@@ -111,44 +153,20 @@ def tile_lowrankconv3d_pa_t_kernel(tc, x_bytes, x_scale, u_k_h, u_k_w, u_k_d, u_
         uout_g = keep.tile([P, CO * T], BF16, name="uout_g", align_bytes=64)
         uout_c = keep.tile([P, CO], U32, name="uout_c", align_bytes=64)
         uout_s = keep.tile([P, CO], U8, name="uout_s", align_bytes=64)
-        nc.vector.tensor_copy(
-            out=uin_g[:].rearrange("p (t m j) -> p t m j", t=T, j=T), in_=uin_raw[:].rearrange("p j (m t) -> p t m j", t=T)
-        )
-        interleave(0, xw0, "v")
-        nc.vector.quantize_mx(out=uin_c[:].bitcast(FP8X4), scales=uin_s[:], in_=uin_g[:])
-        quant_x(0)
+        def quant_weights(t):
+            cols = slice(t * P * T, (t + 1) * P * T)
+            nc.vector.tensor_copy(
+                out=uin_g[:, cols].rearrange("p (m j) -> p m j", j=T),
+                in_=uin_raw[:].rearrange("p j (m t) -> p t m j", t=T)[:, t],
+            )
+            q = slice(t * P, (t + 1) * P)
+            nc.vector.quantize_mx(out=uin_c[:, q].bitcast(FP8X4), scales=uin_s[:, q], in_=uin_g[:, cols])
 
-        hf = keep.tile([P, 3, T], F32, name="hf")
-        wd = keep.tile([P, 3, 2, T], F32, name="wd")
-        mag = keep.tile([P, 3, 2, T], F32, name="mag")
-        low = keep.tile([P, 2, T], F32, name="low")
-        mask = keep.tile([P, 2, T], F32, name="mask")
-        keepb = keep.tile([P, 2, T], F32, name="keepb")
-        mid = keep.tile([P, 2, T], F32, name="mid")
-        rec = keep.tile([P, 2, T], F32, name="rec")
-        ratio = keep.tile([P, 2, 2, T], F32, name="ratio")
-        gain = keep.tile([P, T], F32, name="gain")
-        htap = keep.tile([P, 3, T], F32, name="htap")
-        v = nc.vector
-        v.tensor_copy(out=hf[:], in_=tap_raw[0][:])
-        v.tensor_copy(out=wd[:, :, 0, :], in_=tap_raw[1][:])
-        v.tensor_copy(out=wd[:, :, 1, :], in_=tap_raw[2][:])
-        v.tensor_scalar(mag[:], wd[:], -1.0, None, op0=MULT)
-        v.tensor_tensor(out=mag[:], in0=mag[:], in1=wd[:], op=MAX)
-        v.tensor_tensor(out=low[:], in0=mag[:, 0], in1=mag[:, 1], op=MAX)
-        v.tensor_tensor(out=low[:], in0=low[:], in1=mag[:, 2], op=MAX)
-        v.tensor_scalar(low[:], low[:], 2.0**-80, 2.0**-24, op0=MAX, op1=MULT)
-        v.tensor_tensor(out=mask[:], in0=mag[:, 1], in1=low[:], op=IS_LT)
-        v.tensor_scalar(keepb[:], mask[:], -1.0, 1.0, op0=MULT, op1=ADD)
-        v.tensor_tensor(out=keepb[:], in0=keepb[:], in1=wd[:, 1], op=MULT)
-        v.tensor_tensor(out=mid[:], in0=mask[:], in1=low[:], op=MULT)
-        v.tensor_tensor(out=mid[:], in0=mid[:], in1=keepb[:], op=ADD)
-        v.reciprocal(rec[:], mid[:])
-        v.tensor_tensor(out=gain[:], in0=mid[:, 0], in1=mid[:, 1], op=MULT)
-        v.tensor_tensor(out=ratio[:, 0], in0=wd[:, 0], in1=rec[:], op=MULT)
-        v.tensor_tensor(out=ratio[:, 1], in0=wd[:, 2], in1=rec[:], op=MULT)
-        for k in range(3):
-            v.tensor_tensor(out=htap[:, k, :], in0=hf[:, k, :], in1=gain[:], op=MULT)
+        interleave(0, xw0, "v")
+        quant_weights(0)
+        quant_x(0)
+        for t in range(1, T):
+            quant_weights(t)
 
         def project(c):
             codes, scales = xq.pop(c)
@@ -221,15 +239,30 @@ def tile_lowrankconv3d_pa_t_kernel(tc, x_bytes, x_scale, u_k_h, u_k_w, u_k_d, u_
         def filter_w(u):
             n = unit(u)[1]
             for k, shift in ((0, -1), (1, 1)):
-                for t in range(T):
+                for t in range(1 if u in PE_UNITS else 0, T):
                     dst = t2_at(u, t, 0).rearrange("p (n w) d -> p n w d", n=n)
                     fma(dst, t1_at(u, t, shift), ratio[:, k, 0, t : t + 1], t1_at(u, t, 0) if k == 0 else dst)
+
+        wbank = {}
+
+        def filter_w_pe(u):
+            n = unit(u)[1]
+            bank = psum.tile([P, CH], F32, name="pw", tag="pw", bufs=1)
+            for i, (lhs, shift) in enumerate(((diag[0], -1), (ident, 0), (diag[1], 1))):
+                s = slot(unit(u)[0])
+                o = s * WLINE + D + shift * D
+                rhs = t1[:, 0].rearrange("p s q -> p (s q)")[:, o : o + n * WLINE].rearrange("p (n q) -> p n q", n=n)[:, :, 0:ROW]
+                nc.tensor.matmul(bank[:].rearrange("p (n q) -> p n q", n=n), lhs[:], rhs, start=i == 0, stop=i == 2)
+            wbank[u] = bank
+
+        def evacuate_w(u):
+            nc.scalar.activation(t2_at(u, 0, 0), wbank.pop(u)[:].rearrange("p (r d) -> p r d", d=D), COPY)
 
         zt, gt, t3 = {}, {}, {}
 
         def scale_d(u):
             n = unit(u)[1] * ROW
-            g = work.tile([P, T, CH], F32, name="g", tag="g", bufs=2)
+            g = work.tile([P, T, CH], F32, name="g", tag="g", bufs=3)
             for t in range(T):
                 nc.scalar.activation(
                     g[:, t, 0:n].rearrange("p (r d) -> p r d", d=D), t2_at(u, t, 1), COPY, scale=ratio[:, 1, 1, t : t + 1]
@@ -243,20 +276,15 @@ def tile_lowrankconv3d_pa_t_kernel(tc, x_bytes, x_scale, u_k_h, u_k_w, u_k_d, u_
                 fma(z[:, t, 0:n].rearrange("p (r d) -> p r d", d=D), t2_at(u, t, -1), ratio[:, 0, 1, t : t + 1], t2_at(u, t, 0))
             zt[u] = z
 
-        def finish(u, engine, parts):
-            n = unit(u)[1] * ROW
-            z, g = zt.pop(u), gt.pop(u)
-            y = work.tile([P, CH * T], BF16, name="y", tag="y", bufs=3, align_bytes=64)
-            step = n // parts
-            for i in range(parts):
-                a, e = i * step, (i + 1) * step
-                engine.tensor_tensor(
-                    out=y[:, a * T : e * T].rearrange("p (c i t) -> p c t i", i=4, t=T),
-                    in0=z[:, :, a:e].rearrange("p t (c i) -> p c t i", i=4),
-                    in1=g[:, :, a:e].rearrange("p t (c i) -> p c t i", i=4),
-                    op=ADD,
-                )
-            t3[u] = y
+        def finish(u, engine, a, e):
+            if u not in t3:
+                t3[u] = work.tile([P, CH * T], BF16, name="y", tag="y", bufs=3, align_bytes=64)
+            engine.tensor_tensor(
+                out=t3[u][:, a * T : e * T].rearrange("p (c i t) -> p c t i", i=4, t=T),
+                in0=zt[u][:, :, a:e].rearrange("p t (c i) -> p c t i", i=4),
+                in1=gt[u][:, :, a:e].rearrange("p t (c i) -> p c t i", i=4),
+                op=ADD,
+            )
 
         yq, ot = {}, {}
 
@@ -270,7 +298,7 @@ def tile_lowrankconv3d_pa_t_kernel(tc, x_bytes, x_scale, u_k_h, u_k_w, u_k_d, u_
         def expand(u):
             n = unit(u)[1] * ROW
             codes, scales = yq.pop(u)
-            bank = psum.tile([P, CH], F32, name="po", tag="po", bufs=2)
+            bank = psum.tile([P, CH], F32, name="po", tag="po", bufs=1)
             nc.tensor.matmul_mx(
                 out=bank[:, 0:n],
                 lhsT=uout_c[:].bitcast(FP8X4),
@@ -304,35 +332,53 @@ def tile_lowrankconv3d_pa_t_kernel(tc, x_bytes, x_scale, u_k_h, u_k_w, u_k_d, u_
         nc.vector.tensor_copy(out=uout_g[:].rearrange("p (n j) -> p n j", j=T), in_=uout_raw[:].rearrange("p j n -> p n j"))
         nc.vector.quantize_mx(out=uout_c[:].bitcast(FP8X4), scales=uout_s[:], in_=uout_g[:])
 
+        def share(u):
+            return unit(u)[1] * ROW * GSHARE // 16
+
         for j in range(NCH):
-            if j >= 1:
-                finish(j - 1, nc.gpsimd, 2)
+            if j >= 2:
+                finish(j - 2, nc.gpsimd, 0, share(j - 2))
             filter_h(j)
+            if j >= 2:
+                finish(j - 2, nc.vector, share(j - 2), unit(j - 2)[1] * ROW)
+            if j - 1 in PE_UNITS:
+                evacuate_w(j - 1)
+            if j >= 1:
+                scale_d(j - 1)
             if j + 1 < NCH:
                 project(j + 1)
+            if j in PE_UNITS:
+                filter_w_pe(j)
             if j + 3 < NCH:
-                interleave(j + 3, widen(j + 3), "s")
+                xw = widen(j + 3)
             if j + 1 < NCH:
                 evacuate(j + 1)
+            if j + 3 < NCH:
+                interleave(j + 3, xw, "s")
             filter_w(j)
-            scale_d(j)
             if j == NCH - 1:
                 filter_w(NCH)
+                scale_d(NCH - 1)
                 scale_d(NCH)
-            if j >= 1:
-                quant_t3(j - 1)
-                expand(j - 1)
+            if j >= 2:
+                quant_t3(j - 2)
+                expand(j - 2)
             if j + 2 < NCH:
                 quant_x(j + 2)
-            filter_d(j)
             if j >= 1:
-                store(j - 1)
+                filter_d(j - 1)
+            if j >= 2:
+                store(j - 2)
+        filter_d(NCH - 1)
+        finish(NCH - 2, nc.vector, 0, CH)
         filter_d(NCH)
-        finish(NCH - 1, nc.vector, 1)
-        finish(NCH, nc.vector, 1)
+        quant_t3(NCH - 2)
+        expand(NCH - 2)
+        finish(NCH - 1, nc.vector, 0, CH)
+        finish(NCH, nc.vector, 0, ROW)
         quant_t3(NCH - 1)
         expand(NCH - 1)
         quant_t3(NCH)
         expand(NCH)
-        store(NCH - 1)
-        store(NCH)
+        for u in range(NCH - 2, NCH + 1):
+            store(u)

@@ -28,7 +28,7 @@ NCH = BATCH * CPB
 RING = 12
 WLINE = ROW + D
 DP = D + 4
-GSHARE = 12
+GSHARE = 14
 PE_UNITS = range(2, 12)
 
 FLOPS = 2 * BATCH * VOX * (CI * R + R * CO) + 15 * BATCH * VOX * R

@@ -28,8 +28,8 @@ NCH = BATCH * CPB
 RING = 12
 WLINE = ROW + D
 DP = D + 4
-GSHARE = 14
-PE_UNITS = range(2, 12)
+GPSIMD_COLS = 480
+PE_UNITS = tuple(range(2, 12)) + (NCH,)
 
 FLOPS = 2 * BATCH * VOX * (CI * R + R * CO) + 15 * BATCH * VOX * R
 
@@ -60,16 +60,16 @@ def tile_lowrankconv3d_pa_t_kernel(tc, x_bytes, x_scale, u_k_h, u_k_w, u_k_d, u_
         def load_x(b, c0, c1):
             nc.sync.dma_start(out=xb[b][:, :, c0:c1], in_=x_view[b][:, :, c0:c1])
 
+        load_x(0, 0, CH)
+        nc.scalar.dma_start(out=xs[:], in_=x_scale.rearrange("o (p t) h w d -> p (o t h w d)", t=T))
         for s, u in enumerate((u_k_w, u_k_d)):
-            nc.scalar.dma_start(
+            nc.sync.dma_start(
                 out=wdtaps[:, s, 0 : 3 * T].rearrange("p (k t) -> p k t", t=T), in_=u.rearrange("k (p t) -> p k t", t=T)
             )
-        load_x(0, 0, CH)
         nc.sync.dma_start(out=uin_raw[:], in_=u_c_in.rearrange("(p j) r -> p j r", j=T))
         load_x(0, CH, 2 * CH)
         load_x(0, 2 * CH, 4 * CH)
         load_x(0, 4 * CH, 8 * CH)
-        nc.scalar.dma_start(out=xs[:], in_=x_scale.rearrange("o (p t) h w d -> p (o t h w d)", t=T))
         nc.scalar.dma_start(out=htaps[:], in_=u_k_h.rearrange("k (p t) -> p k t", t=T))
         nc.scalar.dma_start(out=uout_raw[:], in_=u_c_out.rearrange("(p j) n -> p j n", j=T))
         nc.scalar.dma_start(out=bias_sb[:], in_=bias.rearrange("(p o) -> p o", o=1))
@@ -114,6 +114,8 @@ def tile_lowrankconv3d_pa_t_kernel(tc, x_bytes, x_scale, u_k_h, u_k_w, u_k_d, u_
             nc.vector.quantize_mx(out=codes[:].bitcast(FP8X4), scales=scales[:], in_=inter_tiles.pop(c)[:])
             xq[c] = (codes, scales)
 
+        xw0 = widen(0, 2)
+
         mag = keep.tile([P, 2, 3, T], F32, name="mag")
         low = keep.tile([P, 2, T], F32, name="low")
         mask = keep.tile([P, 2, T], F32, name="mask")
@@ -144,7 +146,6 @@ def tile_lowrankconv3d_pa_t_kernel(tc, x_bytes, x_scale, u_k_h, u_k_w, u_k_d, u_
         for i in range(2):
             g.tensor_scalar(diag[i][:], ident[:], ratio[:, i, 0, 0:1], 0.0, op0=MULT, op1=ADD)
 
-        xw0 = widen(0, 2)
         xw1 = widen(1)
 
         uin_g = keep.tile([P, R * T], BF16, name="uin_g", align_bytes=64)
@@ -252,11 +253,11 @@ def tile_lowrankconv3d_pa_t_kernel(tc, x_bytes, x_scale, u_k_h, u_k_w, u_k_d, u_
                 s = slot(unit(u)[0])
                 o = s * WLINE + D + shift * D
                 rhs = t1[:, 0].rearrange("p s q -> p (s q)")[:, o : o + n * WLINE].rearrange("p (n q) -> p n q", n=n)[:, :, 0:ROW]
-                nc.tensor.matmul(bank[:].rearrange("p (n q) -> p n q", n=n), lhs[:], rhs, start=i == 0, stop=i == 2)
+                nc.tensor.matmul(bank[:, 0 : n * ROW].rearrange("p (n q) -> p n q", n=n), lhs[:], rhs, start=i == 0, stop=i == 2)
             wbank[u] = bank
 
         def evacuate_w(u):
-            nc.scalar.activation(t2_at(u, 0, 0), wbank.pop(u)[:].rearrange("p (r d) -> p r d", d=D), COPY)
+            nc.scalar.activation(t2_at(u, 0, 0), wbank.pop(u)[:, 0 : unit(u)[1] * ROW].rearrange("p (r d) -> p r d", d=D), COPY)
 
         zt, gt, t3 = {}, {}, {}
 
@@ -332,15 +333,14 @@ def tile_lowrankconv3d_pa_t_kernel(tc, x_bytes, x_scale, u_k_h, u_k_w, u_k_d, u_
         nc.vector.tensor_copy(out=uout_g[:].rearrange("p (n j) -> p n j", j=T), in_=uout_raw[:].rearrange("p j n -> p n j"))
         nc.vector.quantize_mx(out=uout_c[:].bitcast(FP8X4), scales=uout_s[:], in_=uout_g[:])
 
-        def share(u):
-            return unit(u)[1] * ROW * GSHARE // 16
-
         for j in range(NCH):
             if j >= 2:
-                finish(j - 2, nc.gpsimd, 0, share(j - 2))
+                n = unit(j - 2)[1] * ROW
+                split = min(n, GPSIMD_COLS)
+                finish(j - 2, nc.gpsimd, 0, split)
             filter_h(j)
-            if j >= 2:
-                finish(j - 2, nc.vector, share(j - 2), unit(j - 2)[1] * ROW)
+            if j >= 2 and split < n:
+                finish(j - 2, nc.vector, split, n)
             if j - 1 in PE_UNITS:
                 evacuate_w(j - 1)
             if j >= 1:
@@ -357,8 +357,10 @@ def tile_lowrankconv3d_pa_t_kernel(tc, x_bytes, x_scale, u_k_h, u_k_w, u_k_d, u_
                 interleave(j + 3, xw, "s")
             filter_w(j)
             if j == NCH - 1:
+                filter_w_pe(NCH)
                 filter_w(NCH)
                 scale_d(NCH - 1)
+                evacuate_w(NCH)
                 scale_d(NCH)
             if j >= 2:
                 quant_t3(j - 2)

from contextlib import ExitStack

import concourse.mybir as mybir
from concourse.masks import make_identity

F32 = mybir.dt.float32
BF16 = mybir.dt.bfloat16
U32 = mybir.dt.uint32
U8 = mybir.dt.uint8
FP8 = mybir.dt.float8_e4m3fn
FP8X4 = mybir.dt.float8_e4m3fn_x4
ADD = mybir.AluOpType.add
MULT = mybir.AluOpType.mult
MAX = mybir.AluOpType.max
IS_LT = mybir.AluOpType.is_lt
IS_EQ = mybir.AluOpType.is_equal
COPY = mybir.ActivationFunctionType.Copy
IDENTITY = mybir.ActivationFunctionType.Identity

BATCH, CI, R, CO, H, W, D = 2, 512, 512, 128, 16, 16, 16
P = 128
T = 4
ROW = W * D
VOX = H * ROW
CH = 2 * ROW
CPB = VOX // CH
NCH = BATCH * CPB
RING = 12
WLINE = ROW + D
DP = D + 4
GPSIMD_COLS = 480
PE_UNITS = tuple(range(2, 12)) + (NCH,)

FLOPS = 2 * BATCH * VOX * (CI * R + R * CO) + 15 * BATCH * VOX * R


def slot(row):
    return (row + 1) % RING


def tile_lowrankconv3d_pa_t_kernel(tc, x_bytes, x_scale, u_k_h, u_k_w, u_k_d, u_c_in, u_c_out, bias, out):
    nc = tc.nc
    x_view = x_bytes.rearrange("b (p t) h w d -> b p t (h w d)", t=T)
    out_view = out.rearrange("b o h w d -> b o (h w d)")

    with ExitStack() as ctx:
        keep = ctx.enter_context(tc.tile_pool(name="keep", bufs=1))
        work = ctx.enter_context(tc.tile_pool(name="work", bufs=2))
        psum = ctx.enter_context(tc.psum_pool(name="psum", bufs=2))
        ctx.enter_context(tc.manual_schedule())

        xb = [keep.tile([P, T, VOX], U8, name="xb%d" % b, align_bytes=64) for b in range(BATCH)]
        xs = keep.tile([P, T], F32, name="xs")
        uin_raw = keep.tile([P, T, R], BF16, name="uin_raw")
        uout_raw = keep.tile([P, T, CO], BF16, name="uout_raw")
        htaps = keep.tile([P, 3, T], BF16, name="htaps")
        wdtaps = keep.tile([P, 2, 16], BF16, name="wdtaps")
        bias_sb = keep.tile([P, 1], BF16, name="bias_sb")

        def load_x(b, c0, c1):
            nc.sync.dma_start(out=xb[b][:, :, c0:c1], in_=x_view[b][:, :, c0:c1])

        load_x(0, 0, CH)
        nc.scalar.dma_start(out=xs[:], in_=x_scale.rearrange("o (p t) h w d -> p (o t h w d)", t=T))
        for s, u in enumerate((u_k_w, u_k_d)):
            nc.sync.dma_start(
                out=wdtaps[:, s, 0 : 3 * T].rearrange("p (k t) -> p k t", t=T), in_=u.rearrange("k (p t) -> p k t", t=T)
            )
        nc.sync.dma_start(out=uin_raw[:], in_=u_c_in.rearrange("(p j) r -> p j r", j=T))
        load_x(0, CH, 2 * CH)
        load_x(0, 2 * CH, 4 * CH)
        load_x(0, 4 * CH, 8 * CH)
        nc.scalar.dma_start(out=htaps[:], in_=u_k_h.rearrange("k (p t) -> p k t", t=T))
        nc.scalar.dma_start(out=uout_raw[:], in_=u_c_out.rearrange("(p j) n -> p j n", j=T))
        nc.scalar.dma_start(out=bias_sb[:], in_=bias.rearrange("(p o) -> p o", o=1))
        load_x(1, 0, 4 * CH)
        load_x(1, 4 * CH, 8 * CH)

        t1 = keep.tile([P, T, RING + 1, WLINE], F32, name="t1")
        t2 = [keep.tile([P, T, 34 * DP], F32, name="t2_%d" % i) for i in range(3)]
        nc.gpsimd.memset(t1[:, :, :, 0:D], 0.0)
        for i in range(3):
            nc.gpsimd.memset(t2[i][:].rearrange("p t (r q) -> p t r q", q=DP)[:, :, :, D:DP], 0.0)
        ident = keep.tile([P, P], F32, name="ident")
        make_identity(nc, ident[:])
        warm = keep.tile([P, 2], F32, name="warm")
        nc.vector.memset(warm[:, 0:1], 0.0)
        nc.scalar.activation(warm[:, 1:2], warm[:, 0:1], IDENTITY)

        inter_tiles, xq, banks = {}, {}, {}

        def widen(c, vector_from=T):
            b, c0 = c // CPB, (c % CPB) * CH
            xw = work.tile([P, T, CH], BF16, name="xw", tag="xw", bufs=2)
            for t in range(vector_from, T):
                nc.vector.tensor_scalar(xw[:, t, :], xb[b][:, t, c0 : c0 + CH].bitcast(FP8), xs[:, t : t + 1], None, op0=MULT)
            for t in range(vector_from):
                nc.scalar.activation(xw[:, t, :], xb[b][:, t, c0 : c0 + CH].bitcast(FP8), COPY, scale=xs[:, t : t + 1])
            return xw

        def interleave(c, xw, engine):
            xi = work.tile([P, CH * T], BF16, name="xi", tag="xi", bufs=3, align_bytes=64)
            dst = xi[:].rearrange("p (c i t) -> p c t i", i=4, t=T)
            src = xw[:].rearrange("p t (c i) -> p c t i", i=4)
            if engine == "v":
                nc.vector.tensor_copy(out=dst, in_=src)
            else:
                nc.scalar.copy(dst, src)
            inter_tiles[c] = xi

        def quant_x(c):
            codes = work.tile([P, CH], U32, name="xc", tag="xc", bufs=3, align_bytes=64)
            scales = work.tile([P, CH], U8, name="xsc", tag="xsc", bufs=3, align_bytes=64)
            nc.vector.quantize_mx(out=codes[:].bitcast(FP8X4), scales=scales[:], in_=inter_tiles.pop(c)[:])
            xq[c] = (codes, scales)

        xw0 = widen(0, 2)

        mag = keep.tile([P, 2, 3, T], F32, name="mag")
        low = keep.tile([P, 2, T], F32, name="low")
        mask = keep.tile([P, 2, T], F32, name="mask")
        mid = keep.tile([P, 2, T], F32, name="mid")
        fill = keep.tile([P, 2, T], F32, name="fill")
        rec = keep.tile([P, 2, T], F32, name="rec")
        ratio = keep.tile([P, 2, 2, T], F32, name="ratio")
        gain = keep.tile([P, T], F32, name="gain")
        htap = keep.tile([P, 3, T], F32, name="htap")
        v = nc.vector
        wd = wdtaps[:, :, 0 : 3 * T].rearrange("p s (k t) -> p s k t", t=T)
        for s in range(2):
            v.scalar_tensor_tensor(mag[:, s], wd[:, s], -1.0, wd[:, s], op0=MULT, op1=MAX)
        v.tensor_tensor(out=low[:], in0=mag[:, :, 0], in1=mag[:, :, 2], op=MAX)
        v.tensor_scalar(low[:], low[:], 2.0**-80, 2.0**-24, op0=MAX, op1=MULT)
        v.tensor_tensor(out=mask[:], in0=mag[:, :, 1], in1=low[:], op=IS_LT)
        v.scalar_tensor_tensor(mid[:], mask[:], 0.0, wd[:, :, 1], op0=IS_EQ, op1=MULT)
        v.tensor_tensor(out=fill[:], in0=mask[:], in1=low[:], op=MULT)
        v.tensor_tensor(out=mid[:], in0=mid[:], in1=fill[:], op=ADD)
        v.reciprocal(rec[:], mid[:])
        g = nc.gpsimd
        g.tensor_tensor(out=gain[:], in0=mid[:, 0], in1=mid[:, 1], op=MULT)
        for k in (1, 0, 2):
            g.tensor_tensor(out=htap[:, k, :], in0=htaps[:, k, :], in1=gain[:], op=MULT)
        for i, k in enumerate((0, 2)):
            g.tensor_tensor(out=ratio[:, i], in0=wd[:, :, k], in1=rec[:], op=MULT)
        diag = [keep.tile([P, P], F32, name="diag%d" % i) for i in range(2)]
        for i in range(2):
            g.tensor_scalar(diag[i][:], ident[:], ratio[:, i, 0, 0:1], 0.0, op0=MULT, op1=ADD)

        xw1 = widen(1)

        uin_g = keep.tile([P, R * T], BF16, name="uin_g", align_bytes=64)
        uin_c = keep.tile([P, R], U32, name="uin_c", align_bytes=64)
        uin_s = keep.tile([P, R], U8, name="uin_s", align_bytes=64)
        uout_g = keep.tile([P, CO * T], BF16, name="uout_g", align_bytes=64)
        uout_c = keep.tile([P, CO], U32, name="uout_c", align_bytes=64)
        uout_s = keep.tile([P, CO], U8, name="uout_s", align_bytes=64)
        def quant_weights(t):
            cols = slice(t * P * T, (t + 1) * P * T)
            nc.vector.tensor_copy(
                out=uin_g[:, cols].rearrange("p (m j) -> p m j", j=T),
                in_=uin_raw[:].rearrange("p j (m t) -> p t m j", t=T)[:, t],
            )
            q = slice(t * P, (t + 1) * P)
            nc.vector.quantize_mx(out=uin_c[:, q].bitcast(FP8X4), scales=uin_s[:, q], in_=uin_g[:, cols])

        interleave(0, xw0, "v")
        quant_weights(0)
        quant_x(0)
        for t in range(1, T):
            quant_weights(t)

        def project(c):
            codes, scales = xq.pop(c)
            for t in range(T):
                bank = psum.tile([P, CH], F32, name="t0", tag="t0", bufs=6)
                nc.tensor.matmul_mx(
                    out=bank[:],
                    lhsT=uin_c[:, t * P : (t + 1) * P].bitcast(FP8X4),
                    lhsT_scale=uin_s[:, t * P : (t + 1) * P],
                    rhs=codes[:].bitcast(FP8X4),
                    rhs_scale=scales[:],
                    start=True,
                    stop=True,
                )
                banks[c, t] = bank

        def rows(t, row, n):
            s = slot(row)
            return t1[:, t, s : s + n, D:WLINE]

        def pair(ap, n):
            return ap.rearrange("p (n q) -> p n q", n=n)

        def evacuate(c):
            hb, r0 = c % CPB, 2 * c
            for t in range(T):
                bank = banks[c, t]
                if hb == 0:
                    nc.scalar.activation(rows(t, r0, 1), pair(bank[:, 0:ROW], 1), COPY, scale=htap[:, 1, t : t + 1])
                n = 1 if hb == CPB - 1 else 2
                nc.scalar.activation(rows(t, r0 + 1, n), pair(bank[:, 0 : n * ROW], n), COPY, scale=htap[:, 0, t : t + 1])

        def fma(out_ap, in0, scalar, in1):
            nc.vector.scalar_tensor_tensor(out_ap, in0, scalar, in1, op0=MULT, op1=ADD)

        def filter_h(c):
            hb, r0 = c % CPB, 2 * c
            for t in range(T):
                bank, tap = banks[c, t], htap[:, 1, t : t + 1]
                if hb == 0:
                    todo = [(1, 1)]
                elif slot(r0 + 1) == 0:
                    todo = [(0, 1), (1, 1)]
                else:
                    todo = [(0, 2)]
                for i, n in todo:
                    dst = rows(t, r0 + i, n)
                    fma(dst, pair(bank[:, i * ROW : (i + n) * ROW], n), tap, dst)
            for t in range(T):
                bank, tap = banks.pop((c, t)), htap[:, 2, t : t + 1]
                i, n = (1, 1) if hb == 0 else (0, 2)
                dst = rows(t, r0 - 1 + i, n)
                fma(dst, pair(bank[:, i * ROW : (i + n) * ROW], n), tap, dst)

        def unit(u):
            return (0, 1) if u == 0 else ((2 * u - 1, 1) if u == NCH else (2 * u - 1, 2))

        def t1_at(u, t, shift):
            row, n = unit(u)
            s = slot(row)
            flat = t1[:, t].rearrange("p s q -> p (s q)")
            o = s * WLINE + D + shift * D
            return flat[:, o : o + n * WLINE].rearrange("p (n q) -> p n q", n=n)[:, :, 0:ROW].rearrange("p n (w d) -> p n w d", d=D)

        def t2_at(u, t, shift):
            n = unit(u)[1] * W
            o = DP + shift
            return t2[u % 3][:, t, o : o + n * DP].rearrange("p (n q) -> p n q", q=DP)[:, :, 0:D]

        def filter_w(u):
            n = unit(u)[1]
            for k, shift in ((0, -1), (1, 1)):
                for t in range(1 if u in PE_UNITS else 0, T):
                    dst = t2_at(u, t, 0).rearrange("p (n w) d -> p n w d", n=n)
                    fma(dst, t1_at(u, t, shift), ratio[:, k, 0, t : t + 1], t1_at(u, t, 0) if k == 0 else dst)

        wbank = {}

        def filter_w_pe(u):
            n = unit(u)[1]
            bank = psum.tile([P, CH], F32, name="pw", tag="pw", bufs=1)
            for i, (lhs, shift) in enumerate(((diag[0], -1), (ident, 0), (diag[1], 1))):
                s = slot(unit(u)[0])
                o = s * WLINE + D + shift * D
                rhs = t1[:, 0].rearrange("p s q -> p (s q)")[:, o : o + n * WLINE].rearrange("p (n q) -> p n q", n=n)[:, :, 0:ROW]
                nc.tensor.matmul(bank[:, 0 : n * ROW].rearrange("p (n q) -> p n q", n=n), lhs[:], rhs, start=i == 0, stop=i == 2)
            wbank[u] = bank

        def evacuate_w(u):
            nc.scalar.activation(t2_at(u, 0, 0), wbank.pop(u)[:, 0 : unit(u)[1] * ROW].rearrange("p (r d) -> p r d", d=D), COPY)

        zt, gt, t3 = {}, {}, {}

        def scale_d(u):
            n = unit(u)[1] * ROW
            g = work.tile([P, T, CH], F32, name="g", tag="g", bufs=3)
            for t in range(T):
                nc.scalar.activation(
                    g[:, t, 0:n].rearrange("p (r d) -> p r d", d=D), t2_at(u, t, 1), COPY, scale=ratio[:, 1, 1, t : t + 1]
                )
            gt[u] = g

        def filter_d(u):
            n = unit(u)[1] * ROW
            z = work.tile([P, T, CH], F32, name="z", tag="z", bufs=2)
            for t in range(T):
                fma(z[:, t, 0:n].rearrange("p (r d) -> p r d", d=D), t2_at(u, t, -1), ratio[:, 0, 1, t : t + 1], t2_at(u, t, 0))
            zt[u] = z

        def finish(u, engine, a, e):
            if u not in t3:
                t3[u] = work.tile([P, CH * T], BF16, name="y", tag="y", bufs=3, align_bytes=64)
            engine.tensor_tensor(
                out=t3[u][:, a * T : e * T].rearrange("p (c i t) -> p c t i", i=4, t=T),
                in0=zt[u][:, :, a:e].rearrange("p t (c i) -> p c t i", i=4),
                in1=gt[u][:, :, a:e].rearrange("p t (c i) -> p c t i", i=4),
                op=ADD,
            )

        yq, ot = {}, {}

        def quant_t3(u):
            n = unit(u)[1] * ROW
            codes = work.tile([P, CH], U32, name="yc", tag="yc", bufs=2, align_bytes=64)
            scales = work.tile([P, CH], U8, name="ysc", tag="ysc", bufs=2, align_bytes=64)
            nc.vector.quantize_mx(out=codes[:, 0:n].bitcast(FP8X4), scales=scales[:, 0:n], in_=t3.pop(u)[:, 0 : n * T])
            yq[u] = (codes, scales)

        def expand(u):
            n = unit(u)[1] * ROW
            codes, scales = yq.pop(u)
            bank = psum.tile([P, CH], F32, name="po", tag="po", bufs=1)
            nc.tensor.matmul_mx(
                out=bank[:, 0:n],
                lhsT=uout_c[:].bitcast(FP8X4),
                lhsT_scale=uout_s[:],
                rhs=codes[:, 0:n].bitcast(FP8X4),
                rhs_scale=scales[:, 0:n],
                start=True,
                stop=True,
            )
            ot[u] = bank

        def store(u):
            row, nr = unit(u)
            n = nr * ROW
            bank = ot.pop(u)
            res = work.tile([P, CH], F32, name="res", tag="res", bufs=3)
            nc.scalar.activation(res[:, 0:n], bank[:, 0:n], IDENTITY, bias=bias_sb[:, 0:1])
            groups = {}
            for i in range(nr):
                groups.setdefault((row + i) // H, []).append(i)
            for b, idx in groups.items():
                o = (row + idx[0] - b * H) * ROW
                m = len(idx) * ROW
                nc.sync.dma_start(out=out_view[b][:, o : o + m], in_=res[:, idx[0] * ROW : idx[0] * ROW + m])

        interleave(1, xw1, "v")
        project(0)
        evacuate(0)
        interleave(2, widen(2), "s")
        quant_x(1)
        nc.vector.tensor_copy(out=uout_g[:].rearrange("p (n j) -> p n j", j=T), in_=uout_raw[:].rearrange("p j n -> p n j"))
        nc.vector.quantize_mx(out=uout_c[:].bitcast(FP8X4), scales=uout_s[:], in_=uout_g[:])

        for j in range(NCH):
            if j >= 2:
                n = unit(j - 2)[1] * ROW
                split = min(n, GPSIMD_COLS)
                finish(j - 2, nc.gpsimd, 0, split)
            filter_h(j)
            if j >= 2 and split < n:
                finish(j - 2, nc.vector, split, n)
            if j - 1 in PE_UNITS:
                evacuate_w(j - 1)
            if j >= 1:
                scale_d(j - 1)
            if j + 1 < NCH:
                project(j + 1)
            if j in PE_UNITS:
                filter_w_pe(j)
            if j + 3 < NCH:
                xw = widen(j + 3)
            if j + 1 < NCH:
                evacuate(j + 1)
            if j + 3 < NCH:
                interleave(j + 3, xw, "s")
            filter_w(j)
            if j == NCH - 1:
                filter_w_pe(NCH)
                filter_w(NCH)
                scale_d(NCH - 1)
                evacuate_w(NCH)
                scale_d(NCH)
            if j >= 2:
                quant_t3(j - 2)
                expand(j - 2)
            if j + 2 < NCH:
                quant_x(j + 2)
            if j >= 1:
                filter_d(j - 1)
            if j >= 2:
                store(j - 2)
        filter_d(NCH - 1)
        finish(NCH - 2, nc.vector, 0, CH)
        filter_d(NCH)
        quant_t3(NCH - 2)
        expand(NCH - 2)
        finish(NCH - 1, nc.vector, 0, CH)
        finish(NCH, nc.vector, 0, ROW)
        quant_t3(NCH - 1)
        expand(NCH - 1)
        quant_t3(NCH)
        expand(NCH)
        for u in range(NCH - 2, NCH + 1):
            store(u)
